import numpy as np
import ml_dtypes


def mxq(x, axis, fmt="e4m3"):
    dtype, down = {"e4m3": (ml_dtypes.float8_e4m3fn, 7), "e5m2": (ml_dtypes.float8_e5m2, 14)}[fmt]
    v = np.moveaxis(np.asarray(x, np.float32).astype(ml_dtypes.bfloat16).astype(np.float64), axis, -1)
    blocks = v.reshape(v.shape[:-1] + (-1, 32))
    amax = np.abs(blocks).max(-1, keepdims=True)
    byte = np.maximum(np.where(amax > 0, np.frexp(amax)[1] - 1 + 127, 0) - down, 1)
    scale = np.exp2(byte - 127.0)
    codes = (blocks / scale).astype(np.float32).astype(dtype).astype(np.float64)
    return np.moveaxis((codes * scale).reshape(v.shape), -1, axis)


WIDE = False


def mx_kscale(k):
    if not WIDE:
        return np.ones(k)
    levels = np.array([10, -10, 5, -5, 0])
    a = np.random.permutation(np.resize(levels, k // 512 * 4)).reshape(k // 512, 4)
    idx = np.arange(k)
    return np.exp2(a[idx // 512, idx % 128 // 32])


BF16 = ml_dtypes.bfloat16


def bf(x):
    return np.asarray(x, np.float32).astype(BF16)


def f64(x):
    return np.asarray(x).astype(np.float64)


E, F, H, MID, OUT = 128, 128, 384, 1024, 128
D = 2 * (F + H)
IN = D + 1


def setup_inputs():
    s = mx_kscale(D)
    t = mx_kscale(MID)
    w1 = np.concatenate([np.random.standard_normal((MID, D)) / np.sqrt(D) / s[None, :],
                         np.random.standard_normal((MID, 1)) * 0.5], axis=1) * t[:, None]
    return {"dst_node_feat": bf(np.random.standard_normal((E, F)) * s[:F]),
            "dst_node_hidden": bf(np.random.standard_normal((E, H)) * s[F:F + H]),
            "src_node_feat": bf(np.random.standard_normal((E, F)) * s[F + H:2 * F + H]),
            "src_node_hidden": bf(np.random.standard_normal((E, H)) * s[2 * F + H:]),
            "edge_feat": bf(np.random.standard_normal(E)),
            "W1": bf(w1),
            "b1": bf(np.random.standard_normal(MID) * 0.3 * t),
            "W2": bf(np.random.standard_normal((OUT, MID)) / np.sqrt(MID) / t[None, :]),
            "b2": bf(np.random.standard_normal(OUT) * 0.3)}


def reference(dst_node_feat, dst_node_hidden, src_node_feat, src_node_hidden, edge_feat, W1, b1, W2, b2):
    x = np.concatenate([f64(dst_node_feat), f64(dst_node_hidden), f64(src_node_feat), f64(src_node_hidden),
                        f64(edge_feat)[:, None]], axis=1)
    w1 = f64(W1)
    pre = (mxq(x[:, :D], 1, "e4m3") @ mxq(w1[:, :D], 1, "e4m3").T) + x[:, D:] * w1[:, D] + f64(b1)
    h = np.maximum(pre, 0.0)
    return np.tanh((mxq(h, 1, "e4m3") @ mxq(f64(W2), 1, "e4m3").T) + f64(b2))

@@ -1,0 +1,204 @@
+from contextlib import ExitStack
+
+import concourse.mybir as mybir
+from concourse.masks import make_identity
+
+F32 = mybir.dt.float32
+BF16 = mybir.dt.bfloat16
+U32 = mybir.dt.uint32
+U8 = mybir.dt.uint8
+FP8X4 = mybir.dt.float8_e4m3fn_x4
+ALU = mybir.AluOpType
+ACT = mybir.ActivationFunctionType
+
+P = 128
+PACK = 4
+K_PASS = P * PACK
+NODE = 1024
+MID = 1024
+PASSES = NODE // K_PASS
+HALVES = 2
+BLOCKS = MID // P
+PAIRS = BLOCKS // 2
+W2_STEP = PAIRS // 2
+
+FLOPS = 2 * P * (NODE + 1) * MID + 2 * P * MID * P
+
+
+def tile_edgenetwork_s_kernel(
+    tc,
+    dst_node_feat,
+    dst_node_hidden,
+    src_node_feat,
+    src_node_hidden,
+    edge_feat,
+    W1,
+    b1,
+    W2,
+    b2,
+    out,
+):
+    nc = tc.nc
+    with ExitStack() as ctx:
+        keep = ctx.enter_context(tc.tile_pool(name="keep", bufs=1))
+        w1_pool = ctx.enter_context(tc.tile_pool(name="w1", bufs=BLOCKS))
+        stream = ctx.enter_context(tc.tile_pool(name="stream", bufs=6))
+        flip_banks = ctx.enter_context(tc.psum_pool(name="flip", bufs=4))
+        hidden_banks = ctx.enter_context(tc.psum_pool(name="hidden", bufs=2))
+        single_banks = ctx.enter_context(tc.psum_pool(name="single", bufs=1))
+        ctx.enter_context(tc.manual_schedule())
+
+        identity = keep.tile([P, P], F32)
+        make_identity(nc, identity[:])
+        vectors = keep.tile([P, 4 * P], BF16)
+        nc.vector.memset(vectors[:], 0.0)
+        ones = keep.tile([P, P], BF16)
+        nc.vector.memset(ones[:], 1.0)
+        table_in = keep.tile([P, 1], F32)
+        table_out = keep.tile([P, 1], F32)
+        nc.vector.memset(table_in[:], 0.0)
+        nc.scalar.activation(out=table_out[:], in_=table_in[:], func=ACT.Tanh)
+
+        x_rows = keep.tile([P, NODE], BF16)
+        column = 0
+        for part in (dst_node_feat, dst_node_hidden, src_node_feat, src_node_hidden):
+            width = part.shape[1]
+            nc.sync.dma_start(out=x_rows[:, column : column + width], in_=part)
+            column += width
+
+        w1_blocks = W1.rearrange("(j p r) k -> j r p k", p=P, r=2)
+        w2_rows = keep.tile([P, MID], BF16)
+        w1_rows = []
+        for block in range(BLOCKS):
+            if block == 2 * W2_STEP:
+                nc.sync.dma_start(out=w2_rows[:], in_=W2)
+            rows = w1_pool.tile([P, NODE + 2], BF16, name="w1_rows")
+            nc.sync.dma_start(out=rows[:, 0 : NODE + 1], in_=w1_blocks[block // 2, block % 2])
+            w1_rows.append(rows)
+
+        nc.gpsimd.dma_start(out=vectors[0:1, 2 * P : 3 * P], in_=edge_feat.rearrange("(o e) -> o e", o=1))
+        nc.gpsimd.dma_start(out=vectors[0:PAIRS, 0 : 2 * P], in_=b1.rearrange("(j q) -> j q", q=2 * P))
+        nc.gpsimd.dma_start(out=vectors[0:1, 3 * P : 4 * P], in_=b2.rearrange("(o n) -> o n", o=1))
+
+        def flip(rows):
+            words = rows[:, 0:NODE].bitcast(F32)
+            bank = flip_banks.tile([P, PASSES * HALVES, P], F32)
+            for q in range(PASSES * HALVES):
+                nc.tensor.transpose(bank[:, q, :], words[:, q * P : (q + 1) * P], identity[:])
+            grouped = stream.tile([P, PASSES, P, PACK], BF16, align_bytes=64)
+            nc.scalar.copy(
+                out=grouped[:].bitcast(F32),
+                in_=bank[:].rearrange("p (g u) c -> p g c u", u=HALVES),
+            )
+            return grouped
+
+        def quantise(grouped, pool, name):
+            codes = pool.tile([P, PASSES * P], U32, name=name + "_codes", align_bytes=64)
+            scales = pool.tile([P, PASSES * P], U8, name=name + "_scales", align_bytes=64)
+            nc.vector.quantize_mx(
+                out=codes[:].bitcast(FP8X4),
+                scales=scales[:],
+                in_=grouped[:].rearrange("p g c t -> p (g c t)"),
+            )
+            return codes, scales
+
+        def multiply(pair):
+            operands = [quantise(turned_w1[2 * pair + r], stream, "w1") for r in range(2)]
+            acc = hidden_banks.tile([P, 2, P], F32, name="hidden_acc")
+            for r in range(2):
+                w1_codes, w1_scales = operands[r]
+                for g in range(PASSES):
+                    cols = slice(g * P, (g + 1) * P)
+                    nc.tensor.matmul_mx(
+                        out=acc[:, r, :],
+                        lhsT=w1_codes[:, cols].bitcast(FP8X4),
+                        lhsT_scale=w1_scales[:, cols],
+                        rhs=x_codes[:, cols].bitcast(FP8X4),
+                        rhs_scale=x_scales[:, cols],
+                        start=(g == 0),
+                        stop=(g == PASSES - 1),
+                    )
+            hidden_acc[pair] = acc
+
+        def spread_vectors():
+            bank = single_banks.tile([P, 3 * P], F32, name="vector_bank")
+            nc.tensor.transpose(bank[:, 0:P], vectors[:, 0 : 2 * P].bitcast(F32), identity[:])
+            nc.tensor.matmul(out=bank[:, P : 3 * P], lhsT=ones[:], rhs=vectors[:, 2 * P : 4 * P], start=True, stop=True)
+            nc.vector.tensor_copy(out=b1_cols[:], in_=bank[:, 0:PAIRS].bitcast(BF16))
+            nc.vector.tensor_copy(out=spread[:], in_=bank[:, P : 3 * P])
+
+        def activate(pair):
+            c, u = divmod(pair, HALVES)
+            sums = []
+            for r in range(2):
+                pre = stream.tile([P, P], F32, name="pre")
+                nc.vector.scalar_tensor_tensor(
+                    out=pre[:],
+                    in0=spread[:, 0:P],
+                    scalar=w1_rows[2 * pair + r][:, NODE : NODE + 1],
+                    in1=hidden_acc[pair][:, r, :],
+                    op0=ALU.mult,
+                    op1=ALU.add,
+                )
+                sums.append(pre)
+            for r in range(2):
+                block = 2 * pair + r
+                nc.vector.tensor_scalar(
+                    out=h_grouped[:, c, :, HALVES * u + r],
+                    in0=sums[r][:],
+                    scalar1=b1_cols[:, block : block + 1],
+                    scalar2=0.0,
+                    op0=ALU.add,
+                    op1=ALU.max,
+                )
+
+        def second_layer_pass(c):
+            cols = slice(c * P, (c + 1) * P)
+            nc.vector.quantize_mx(
+                out=h_codes[:, cols].bitcast(FP8X4),
+                scales=h_scales[:, cols],
+                in_=h_grouped[:, c, :, :].rearrange("p e t -> p (e t)"),
+            )
+            nc.tensor.matmul_mx(
+                out=out_acc[:],
+                lhsT=h_codes[:, cols].bitcast(FP8X4),
+                lhsT_scale=h_scales[:, cols],
+                rhs=w2_codes[:, cols].bitcast(FP8X4),
+                rhs_scale=w2_scales[:, cols],
+                start=(c == 0),
+                stop=(c == PASSES - 1),
+            )
+
+        b1_cols = keep.tile([P, BLOCKS], F32)
+        spread = keep.tile([P, 2 * P], F32)
+        h_grouped = keep.tile([P, PASSES, P, PACK], BF16, align_bytes=64)
+        h_codes = keep.tile([P, PASSES * P], U32, align_bytes=64)
+        h_scales = keep.tile([P, PASSES * P], U8, align_bytes=64)
+        out_acc = single_banks.tile([P, P], F32)
+        turned_w1 = {}
+        hidden_acc = {}
+
+        x_codes, x_scales = quantise(flip(x_rows), keep, "x")
+
+        for step in range(PAIRS + 2):
+            if step == W2_STEP:
+                turned_w2 = flip(w2_rows)
+            if step < PAIRS:
+                for r in range(2):
+                    turned_w1[2 * step + r] = flip(w1_rows[2 * step + r])
+            if 1 <= step <= PAIRS:
+                multiply(step - 1)
+            if step == 1:
+                spread_vectors()
+            if step >= 2:
+                activate(step - 2)
+                if (step - 2) % HALVES == HALVES - 1:
+                    second_layer_pass((step - 2) // HALVES)
+            if step == W2_STEP:
+                w2_codes, w2_scales = quantise(turned_w2, keep, "w2")
+
+        biased = keep.tile([P, P], F32)
+        nc.vector.tensor_tensor(out=biased[:], in0=out_acc[:], in1=spread[:, P : 2 * P], op=ALU.add)
+        result = keep.tile([P, P], F32)
+        nc.scalar.activation(out=result[:], in_=biased[:], func=ACT.Tanh)
+        nc.sync.dma_start(out=out, in_=result[:])

@@ -41,7 +41,7 @@ def tile_edgenetwork_s_kernel(
     nc = tc.nc
     with ExitStack() as ctx:
         keep = ctx.enter_context(tc.tile_pool(name="keep", bufs=1))
-        w1_pool = ctx.enter_context(tc.tile_pool(name="w1", bufs=BLOCKS))
+        w1_pool = ctx.enter_context(tc.tile_pool(name="w1", bufs=PAIRS))
         stream = ctx.enter_context(tc.tile_pool(name="stream", bufs=6))
         flip_banks = ctx.enter_context(tc.psum_pool(name="flip", bufs=4))
         hidden_banks = ctx.enter_context(tc.psum_pool(name="hidden", bufs=2))
@@ -49,7 +49,8 @@ def tile_edgenetwork_s_kernel(
         ctx.enter_context(tc.manual_schedule())
 
         identity = keep.tile([P, P], F32)
-        make_identity(nc, identity[:])
+        nc.vector.memset(identity[:], 0.0)
+        make_identity(nc, identity[:], nomemset=True)
         vectors = keep.tile([P, 4 * P], BF16)
         nc.vector.memset(vectors[:], 0.0)
         ones = keep.tile([P, P], BF16)
@@ -65,23 +66,22 @@ def tile_edgenetwork_s_kernel(
             width = part.shape[1]
             nc.sync.dma_start(out=x_rows[:, column : column + width], in_=part)
             column += width
-
-        w1_blocks = W1.rearrange("(j p r) k -> j r p k", p=P, r=2)
-        w2_rows = keep.tile([P, MID], BF16)
-        w1_rows = []
-        for block in range(BLOCKS):
-            if block == 2 * W2_STEP:
-                nc.sync.dma_start(out=w2_rows[:], in_=W2)
-            rows = w1_pool.tile([P, NODE + 2], BF16, name="w1_rows")
-            nc.sync.dma_start(out=rows[:, 0 : NODE + 1], in_=w1_blocks[block // 2, block % 2])
-            w1_rows.append(rows)
-
-        nc.gpsimd.dma_start(out=vectors[0:1, 2 * P : 3 * P], in_=edge_feat.rearrange("(o e) -> o e", o=1))
-        nc.gpsimd.dma_start(out=vectors[0:PAIRS, 0 : 2 * P], in_=b1.rearrange("(j q) -> j q", q=2 * P))
+        nc.sync.dma_start(out=vectors[0:1, 2 * P : 3 * P], in_=edge_feat.rearrange("(o e) -> o e", o=1))
+        nc.sync.dma_start(out=vectors[0:PAIRS, 0 : 2 * P], in_=b1.rearrange("(j q) -> j q", q=2 * P))
         nc.gpsimd.dma_start(out=vectors[0:1, 3 * P : 4 * P], in_=b2.rearrange("(o n) -> o n", o=1))
 
+        w1_pairs = W1.rearrange("(j p r) k -> j p r k", p=P, r=2)
+        w2_rows = keep.tile([P, MID], BF16)
+        w1_rows = []
+        for pair in range(PAIRS):
+            if pair == W2_STEP:
+                nc.sync.dma_start(out=w2_rows[:], in_=W2)
+            rows = w1_pool.tile([P, 2, NODE + 2], BF16, name="w1_rows")
+            nc.sync.dma_start(out=rows[:, :, 0 : NODE + 1], in_=w1_pairs[pair])
+            w1_rows.append(rows)
+
         def flip(rows):
-            words = rows[:, 0:NODE].bitcast(F32)
+            words = rows.bitcast(F32)
             bank = flip_banks.tile([P, PASSES * HALVES, P], F32)
             for q in range(PASSES * HALVES):
                 nc.tensor.transpose(bank[:, q, :], words[:, q * P : (q + 1) * P], identity[:])
@@ -119,41 +119,42 @@ def tile_edgenetwork_s_kernel(
                         stop=(g == PASSES - 1),
                     )
             hidden_acc[pair] = acc
+            terms = stream.tile([P, 2, P], F32, name="edge_terms")
+            for r in range(2):
+                block = 2 * pair + r
+                nc.vector.tensor_scalar(
+                    out=terms[:, r, :],
+                    in0=spread[:, 0:P],
+                    scalar1=w1_rows[pair][:, r, NODE : NODE + 1],
+                    scalar2=b1_cols[:, block : block + 1],
+                    op0=ALU.mult,
+                    op1=ALU.add,
+                )
+            edge_terms[pair] = terms
 
         def spread_vectors():
             bank = single_banks.tile([P, 3 * P], F32, name="vector_bank")
             nc.tensor.transpose(bank[:, 0:P], vectors[:, 0 : 2 * P].bitcast(F32), identity[:])
             nc.tensor.matmul(out=bank[:, P : 3 * P], lhsT=ones[:], rhs=vectors[:, 2 * P : 4 * P], start=True, stop=True)
-            nc.vector.tensor_copy(out=b1_cols[:], in_=bank[:, 0:PAIRS].bitcast(BF16))
-            nc.vector.tensor_copy(out=spread[:], in_=bank[:, P : 3 * P])
+            nc.scalar.copy(out=b1_cols[:], in_=bank[:, 0:PAIRS].bitcast(BF16))
+            nc.scalar.copy(out=spread[:], in_=bank[:, P : 3 * P])
 
-        def activate(pair):
+        def add_edge_terms(pair):
             c, u = divmod(pair, HALVES)
-            sums = []
-            for r in range(2):
-                pre = stream.tile([P, P], F32, name="pre")
-                nc.vector.scalar_tensor_tensor(
-                    out=pre[:],
-                    in0=spread[:, 0:P],
-                    scalar=w1_rows[2 * pair + r][:, NODE : NODE + 1],
-                    in1=hidden_acc[pair][:, r, :],
-                    op0=ALU.mult,
-                    op1=ALU.add,
-                )
-                sums.append(pre)
-            for r in range(2):
-                block = 2 * pair + r
-                nc.vector.tensor_scalar(
-                    out=h_grouped[:, c, :, HALVES * u + r],
-                    in0=sums[r][:],
-                    scalar1=b1_cols[:, block : block + 1],
-                    scalar2=0.0,
-                    op0=ALU.add,
-                    op1=ALU.max,
-                )
+            nc.vector.tensor_tensor(
+                out=pre[:, c, HALVES * u : HALVES * u + 2, :],
+                in0=hidden_acc[pair][:],
+                in1=edge_terms[pair][:],
+                op=ALU.add,
+            )
 
         def second_layer_pass(c):
             cols = slice(c * P, (c + 1) * P)
+            nc.vector.tensor_scalar_max(
+                out=h_grouped[:, c, :, :],
+                in0=pre[:, c, :, :].rearrange("p t e -> p e t"),
+                scalar1=0.0,
+            )
             nc.vector.quantize_mx(
                 out=h_codes[:, cols].bitcast(FP8X4),
                 scales=h_scales[:, cols],
@@ -169,29 +170,31 @@ def tile_edgenetwork_s_kernel(
                 stop=(c == PASSES - 1),
             )
 
-        b1_cols = keep.tile([P, BLOCKS], F32)
+        b1_cols = keep.tile([P, BLOCKS], BF16)
         spread = keep.tile([P, 2 * P], F32)
+        pre = keep.tile([P, PASSES, PACK, P], F32)
         h_grouped = keep.tile([P, PASSES, P, PACK], BF16, align_bytes=64)
         h_codes = keep.tile([P, PASSES * P], U32, align_bytes=64)
         h_scales = keep.tile([P, PASSES * P], U8, align_bytes=64)
         out_acc = single_banks.tile([P, P], F32)
         turned_w1 = {}
         hidden_acc = {}
+        edge_terms = {}
 
-        x_codes, x_scales = quantise(flip(x_rows), keep, "x")
+        x_codes, x_scales = quantise(flip(x_rows[:]), keep, "x")
 
         for step in range(PAIRS + 2):
             if step == W2_STEP:
-                turned_w2 = flip(w2_rows)
+                turned_w2 = flip(w2_rows[:])
             if step < PAIRS:
                 for r in range(2):
-                    turned_w1[2 * step + r] = flip(w1_rows[2 * step + r])
+                    turned_w1[2 * step + r] = flip(w1_rows[step][:, r, 0:NODE])
+            if step == 0:
+                spread_vectors()
             if 1 <= step <= PAIRS:
                 multiply(step - 1)
-            if step == 1:
-                spread_vectors()
             if step >= 2:
-                activate(step - 2)
+                add_edge_terms(step - 2)
                 if (step - 2) % HALVES == HALVES - 1:
                     second_layer_pass((step - 2) // HALVES)
             if step == W2_STEP:

@@ -20,7 +20,9 @@ PASSES = NODE // K_PASS
 HALVES = 2
 BLOCKS = MID // P
 PAIRS = BLOCKS // 2
-W2_STEP = PAIRS // 2
+N_IDLE = 256
+IDLE_BEFORE_X = 12
+IDLE_AFTER_X = 6
 
 FLOPS = 2 * P * (NODE + 1) * MID + 2 * P * MID * P
 
@@ -48,11 +50,16 @@ def tile_edgenetwork_s_kernel(
         single_banks = ctx.enter_context(tc.psum_pool(name="single", bufs=1))
         ctx.enter_context(tc.manual_schedule())
 
+        vectors = keep.tile([P, 4 * P], BF16)
+        nc.vector.memset(vectors[:], 0.0)
+        zeros = keep.tile([P, PACK * N_IDLE], BF16, align_bytes=64)
+        idle_codes = keep.tile([P, N_IDLE], U32, align_bytes=64)
+        idle_scales = keep.tile([P, N_IDLE], U8, align_bytes=64)
+        nc.vector.memset(zeros[:], 0.0)
+        nc.vector.quantize_mx(out=idle_codes[:].bitcast(FP8X4), scales=idle_scales[:], in_=zeros[:])
         identity = keep.tile([P, P], F32)
         nc.vector.memset(identity[:], 0.0)
         make_identity(nc, identity[:], nomemset=True)
-        vectors = keep.tile([P, 4 * P], BF16)
-        nc.vector.memset(vectors[:], 0.0)
         ones = keep.tile([P, P], BF16)
         nc.vector.memset(ones[:], 1.0)
         table_in = keep.tile([P, 1], F32)
@@ -68,17 +75,16 @@ def tile_edgenetwork_s_kernel(
             column += width
         nc.sync.dma_start(out=vectors[0:1, 2 * P : 3 * P], in_=edge_feat.rearrange("(o e) -> o e", o=1))
         nc.sync.dma_start(out=vectors[0:PAIRS, 0 : 2 * P], in_=b1.rearrange("(j q) -> j q", q=2 * P))
-        nc.gpsimd.dma_start(out=vectors[0:1, 3 * P : 4 * P], in_=b2.rearrange("(o n) -> o n", o=1))
 
         w1_pairs = W1.rearrange("(j p r) k -> j p r k", p=P, r=2)
-        w2_rows = keep.tile([P, MID], BF16)
         w1_rows = []
         for pair in range(PAIRS):
-            if pair == W2_STEP:
-                nc.sync.dma_start(out=w2_rows[:], in_=W2)
             rows = w1_pool.tile([P, 2, NODE + 2], BF16, name="w1_rows")
             nc.sync.dma_start(out=rows[:, :, 0 : NODE + 1], in_=w1_pairs[pair])
             w1_rows.append(rows)
+        w2_rows = keep.tile([P, MID], BF16)
+        nc.sync.dma_start(out=w2_rows[:], in_=W2)
+        nc.sync.dma_start(out=vectors[0:1, 3 * P : 4 * P], in_=b2.rearrange("(o n) -> o n", o=1))
 
         def flip(rows):
             words = rows.bitcast(F32)
@@ -119,6 +125,8 @@ def tile_edgenetwork_s_kernel(
                         stop=(g == PASSES - 1),
                     )
             hidden_acc[pair] = acc
+
+        def edge_and_bias(pair):
             terms = stream.tile([P, 2, P], F32, name="edge_terms")
             for r in range(2):
                 block = 2 * pair + r
@@ -132,12 +140,19 @@ def tile_edgenetwork_s_kernel(
                 )
             edge_terms[pair] = terms
 
-        def spread_vectors():
-            bank = single_banks.tile([P, 3 * P], F32, name="vector_bank")
-            nc.tensor.transpose(bank[:, 0:P], vectors[:, 0 : 2 * P].bitcast(F32), identity[:])
-            nc.tensor.matmul(out=bank[:, P : 3 * P], lhsT=ones[:], rhs=vectors[:, 2 * P : 4 * P], start=True, stop=True)
-            nc.scalar.copy(out=b1_cols[:], in_=bank[:, 0:PAIRS].bitcast(BF16))
-            nc.scalar.copy(out=spread[:], in_=bank[:, P : 3 * P])
+        def spread_row(part):
+            nc.tensor.matmul(
+                out=vector_bank[:, (1 + part) * P : (2 + part) * P],
+                lhsT=ones[:],
+                rhs=vectors[:, (2 + part) * P : (3 + part) * P],
+                start=True,
+                stop=True,
+            )
+            nc.scalar.copy(out=spread[:, part * P : (part + 1) * P], in_=vector_bank[:, (1 + part) * P : (2 + part) * P])
+
+        def turn_b1():
+            nc.tensor.transpose(vector_bank[:, 0:P], vectors[:, 0 : 2 * P].bitcast(F32), identity[:])
+            nc.scalar.copy(out=b1_cols[:], in_=vector_bank[:, 0:PAIRS].bitcast(BF16))
 
         def add_edge_terms(pair):
             c, u = divmod(pair, HALVES)
@@ -148,7 +163,7 @@ def tile_edgenetwork_s_kernel(
                 op=ALU.add,
             )
 
-        def second_layer_pass(c):
+        def hidden_pass(c):
             cols = slice(c * P, (c + 1) * P)
             nc.vector.tensor_scalar_max(
                 out=h_grouped[:, c, :, :],
@@ -160,6 +175,58 @@ def tile_edgenetwork_s_kernel(
                 scales=h_scales[:, cols],
                 in_=h_grouped[:, c, :, :].rearrange("p e t -> p (e t)"),
             )
+
+        def idle_passes(count):
+            for i in range(count):
+                nc.tensor.matmul_mx(
+                    out=idle_bank[:],
+                    lhsT=idle_codes[:, 0:P].bitcast(FP8X4),
+                    lhsT_scale=idle_scales[:, 0:P],
+                    rhs=idle_codes[:].bitcast(FP8X4),
+                    rhs_scale=idle_scales[:],
+                    start=True,
+                    stop=True,
+                )
+
+        b1_cols = keep.tile([P, BLOCKS], BF16)
+        spread = keep.tile([P, 2 * P], F32)
+        pre = keep.tile([P, PASSES, PACK, P], F32)
+        h_grouped = keep.tile([P, PASSES, P, PACK], BF16, align_bytes=64)
+        h_codes = keep.tile([P, PASSES * P], U32, align_bytes=64)
+        h_scales = keep.tile([P, PASSES * P], U8, align_bytes=64)
+        out_acc = single_banks.tile([P, P], F32)
+        vector_bank = single_banks.tile([P, 3 * P], F32)
+        idle_bank = flip_banks.tile([P, N_IDLE], F32, name="bank")
+        turned_w1 = {}
+        hidden_acc = {}
+        edge_terms = {}
+
+        idle_passes(IDLE_BEFORE_X)
+        x_codes, x_scales = quantise(flip(x_rows[:]), keep, "x")
+        turn_b1()
+        spread_row(0)
+        idle_passes(IDLE_AFTER_X)
+
+        for step in range(PAIRS + 2):
+            if step < PAIRS:
+                for r in range(2):
+                    turned_w1[2 * step + r] = flip(w1_rows[step][:, r, 0:NODE])
+            if step == PAIRS:
+                turned_w2 = flip(w2_rows[:])
+                spread_row(1)
+            if 1 <= step <= PAIRS:
+                multiply(step - 1)
+            if step < PAIRS:
+                edge_and_bias(step)
+            if step >= 2:
+                add_edge_terms(step - 2)
+                if (step - 2) % HALVES == HALVES - 1:
+                    hidden_pass((step - 2) // HALVES)
+            if step == PAIRS:
+                w2_codes, w2_scales = quantise(turned_w2, keep, "w2")
+
+        for c in range(PASSES):
+            cols = slice(c * P, (c + 1) * P)
             nc.tensor.matmul_mx(
                 out=out_acc[:],
                 lhsT=h_codes[:, cols].bitcast(FP8X4),
@@ -169,36 +236,6 @@ def tile_edgenetwork_s_kernel(
                 start=(c == 0),
                 stop=(c == PASSES - 1),
             )
-
-        b1_cols = keep.tile([P, BLOCKS], BF16)
-        spread = keep.tile([P, 2 * P], F32)
-        pre = keep.tile([P, PASSES, PACK, P], F32)
-        h_grouped = keep.tile([P, PASSES, P, PACK], BF16, align_bytes=64)
-        h_codes = keep.tile([P, PASSES * P], U32, align_bytes=64)
-        h_scales = keep.tile([P, PASSES * P], U8, align_bytes=64)
-        out_acc = single_banks.tile([P, P], F32)
-        turned_w1 = {}
-        hidden_acc = {}
-        edge_terms = {}
-
-        x_codes, x_scales = quantise(flip(x_rows[:]), keep, "x")
-
-        for step in range(PAIRS + 2):
-            if step == W2_STEP:
-                turned_w2 = flip(w2_rows[:])
-            if step < PAIRS:
-                for r in range(2):
-                    turned_w1[2 * step + r] = flip(w1_rows[step][:, r, 0:NODE])
-            if step == 0:
-                spread_vectors()
-            if 1 <= step <= PAIRS:
-                multiply(step - 1)
-            if step >= 2:
-                add_edge_terms(step - 2)
-                if (step - 2) % HALVES == HALVES - 1:
-                    second_layer_pass((step - 2) // HALVES)
-            if step == W2_STEP:
-                w2_codes, w2_scales = quantise(turned_w2, keep, "w2")
 
         biased = keep.tile([P, P], F32)
         nc.vector.tensor_tensor(out=biased[:], in0=out_acc[:], in1=spread[:, P : 2 * P], op=ALU.add)

from contextlib import ExitStack

import concourse.mybir as mybir
from concourse.masks import make_identity

F32 = mybir.dt.float32
BF16 = mybir.dt.bfloat16
U32 = mybir.dt.uint32
U8 = mybir.dt.uint8
FP8X4 = mybir.dt.float8_e4m3fn_x4
ALU = mybir.AluOpType
ACT = mybir.ActivationFunctionType

P = 128
PACK = 4
K_PASS = P * PACK
NODE = 1024
MID = 1024
PASSES = NODE // K_PASS
HALVES = 2
BLOCKS = MID // P
PAIRS = BLOCKS // 2
N_IDLE = 256
IDLE_BEFORE_X = 12
IDLE_AFTER_X = 6

FLOPS = 2 * P * (NODE + 1) * MID + 2 * P * MID * P


def tile_edgenetwork_s_kernel(
    tc,
    dst_node_feat,
    dst_node_hidden,
    src_node_feat,
    src_node_hidden,
    edge_feat,
    W1,
    b1,
    W2,
    b2,
    out,
):
    nc = tc.nc
    with ExitStack() as ctx:
        keep = ctx.enter_context(tc.tile_pool(name="keep", bufs=1))
        w1_pool = ctx.enter_context(tc.tile_pool(name="w1", bufs=PAIRS))
        stream = ctx.enter_context(tc.tile_pool(name="stream", bufs=6))
        flip_banks = ctx.enter_context(tc.psum_pool(name="flip", bufs=4))
        hidden_banks = ctx.enter_context(tc.psum_pool(name="hidden", bufs=2))
        single_banks = ctx.enter_context(tc.psum_pool(name="single", bufs=1))
        ctx.enter_context(tc.manual_schedule())

        vectors = keep.tile([P, 4 * P], BF16)
        nc.vector.memset(vectors[:], 0.0)
        zeros = keep.tile([P, PACK * N_IDLE], BF16, align_bytes=64)
        idle_codes = keep.tile([P, N_IDLE], U32, align_bytes=64)
        idle_scales = keep.tile([P, N_IDLE], U8, align_bytes=64)
        nc.vector.memset(zeros[:], 0.0)
        nc.vector.quantize_mx(out=idle_codes[:].bitcast(FP8X4), scales=idle_scales[:], in_=zeros[:])
        identity = keep.tile([P, P], F32)
        nc.vector.memset(identity[:], 0.0)
        make_identity(nc, identity[:], nomemset=True)
        ones = keep.tile([P, P], BF16)
        nc.vector.memset(ones[:], 1.0)
        table_in = keep.tile([P, 1], F32)
        table_out = keep.tile([P, 1], F32)
        nc.vector.memset(table_in[:], 0.0)
        nc.scalar.activation(out=table_out[:], in_=table_in[:], func=ACT.Tanh)

        x_rows = keep.tile([P, NODE], BF16)
        column = 0
        for part in (dst_node_feat, dst_node_hidden, src_node_feat, src_node_hidden):
            width = part.shape[1]
            nc.sync.dma_start(out=x_rows[:, column : column + width], in_=part)
            column += width
        nc.sync.dma_start(out=vectors[0:1, 2 * P : 3 * P], in_=edge_feat.rearrange("(o e) -> o e", o=1))
        nc.sync.dma_start(out=vectors[0:PAIRS, 0 : 2 * P], in_=b1.rearrange("(j q) -> j q", q=2 * P))

        w1_pairs = W1.rearrange("(j p r) k -> j p r k", p=P, r=2)
        w1_rows = []
        for pair in range(PAIRS):
            rows = w1_pool.tile([P, 2, NODE + 2], BF16, name="w1_rows")
            nc.sync.dma_start(out=rows[:, :, 0 : NODE + 1], in_=w1_pairs[pair])
            w1_rows.append(rows)
        w2_rows = keep.tile([P, MID], BF16)
        nc.sync.dma_start(out=w2_rows[:], in_=W2)
        nc.sync.dma_start(out=vectors[0:1, 3 * P : 4 * P], in_=b2.rearrange("(o n) -> o n", o=1))

        def flip(rows):
            words = rows.bitcast(F32)
            bank = flip_banks.tile([P, PASSES * HALVES, P], F32)
            for q in range(PASSES * HALVES):
                nc.tensor.transpose(bank[:, q, :], words[:, q * P : (q + 1) * P], identity[:])
            grouped = stream.tile([P, PASSES, P, PACK], BF16, align_bytes=64)
            nc.scalar.copy(
                out=grouped[:].bitcast(F32),
                in_=bank[:].rearrange("p (g u) c -> p g c u", u=HALVES),
            )
            return grouped

        def quantise(grouped, pool, name):
            codes = pool.tile([P, PASSES * P], U32, name=name + "_codes", align_bytes=64)
            scales = pool.tile([P, PASSES * P], U8, name=name + "_scales", align_bytes=64)
            nc.vector.quantize_mx(
                out=codes[:].bitcast(FP8X4),
                scales=scales[:],
                in_=grouped[:].rearrange("p g c t -> p (g c t)"),
            )
            return codes, scales

        def multiply(pair):
            operands = [quantise(turned_w1[2 * pair + r], stream, "w1") for r in range(2)]
            acc = hidden_banks.tile([P, 2, P], F32, name="hidden_acc")
            for r in range(2):
                w1_codes, w1_scales = operands[r]
                for g in range(PASSES):
                    cols = slice(g * P, (g + 1) * P)
                    nc.tensor.matmul_mx(
                        out=acc[:, r, :],
                        lhsT=w1_codes[:, cols].bitcast(FP8X4),
                        lhsT_scale=w1_scales[:, cols],
                        rhs=x_codes[:, cols].bitcast(FP8X4),
                        rhs_scale=x_scales[:, cols],
                        start=(g == 0),
                        stop=(g == PASSES - 1),
                    )
            hidden_acc[pair] = acc

        def edge_and_bias(pair):
            terms = stream.tile([P, 2, P], F32, name="edge_terms")
            for r in range(2):
                block = 2 * pair + r
                nc.vector.tensor_scalar(
                    out=terms[:, r, :],
                    in0=spread[:, 0:P],
                    scalar1=w1_rows[pair][:, r, NODE : NODE + 1],
                    scalar2=b1_cols[:, block : block + 1],
                    op0=ALU.mult,
                    op1=ALU.add,
                )
            edge_terms[pair] = terms

        def spread_row(part):
            nc.tensor.matmul(
                out=vector_bank[:, (1 + part) * P : (2 + part) * P],
                lhsT=ones[:],
                rhs=vectors[:, (2 + part) * P : (3 + part) * P],
                start=True,
                stop=True,
            )
            nc.scalar.copy(out=spread[:, part * P : (part + 1) * P], in_=vector_bank[:, (1 + part) * P : (2 + part) * P])

        def turn_b1():
            nc.tensor.transpose(vector_bank[:, 0:P], vectors[:, 0 : 2 * P].bitcast(F32), identity[:])
            nc.scalar.copy(out=b1_cols[:], in_=vector_bank[:, 0:PAIRS].bitcast(BF16))

        def add_edge_terms(pair):
            c, u = divmod(pair, HALVES)
            nc.vector.tensor_tensor(
                out=pre[:, c, HALVES * u : HALVES * u + 2, :],
                in0=hidden_acc[pair][:],
                in1=edge_terms[pair][:],
                op=ALU.add,
            )

        def hidden_pass(c):
            cols = slice(c * P, (c + 1) * P)
            nc.vector.tensor_scalar_max(
                out=h_grouped[:, c, :, :],
                in0=pre[:, c, :, :].rearrange("p t e -> p e t"),
                scalar1=0.0,
            )
            nc.vector.quantize_mx(
                out=h_codes[:, cols].bitcast(FP8X4),
                scales=h_scales[:, cols],
                in_=h_grouped[:, c, :, :].rearrange("p e t -> p (e t)"),
            )

        def idle_passes(count):
            for i in range(count):
                nc.tensor.matmul_mx(
                    out=idle_bank[:],
                    lhsT=idle_codes[:, 0:P].bitcast(FP8X4),
                    lhsT_scale=idle_scales[:, 0:P],
                    rhs=idle_codes[:].bitcast(FP8X4),
                    rhs_scale=idle_scales[:],
                    start=True,
                    stop=True,
                )

        b1_cols = keep.tile([P, BLOCKS], BF16)
        spread = keep.tile([P, 2 * P], F32)
        pre = keep.tile([P, PASSES, PACK, P], F32)
        h_grouped = keep.tile([P, PASSES, P, PACK], BF16, align_bytes=64)
        h_codes = keep.tile([P, PASSES * P], U32, align_bytes=64)
        h_scales = keep.tile([P, PASSES * P], U8, align_bytes=64)
        out_acc = single_banks.tile([P, P], F32)
        vector_bank = single_banks.tile([P, 3 * P], F32)
        idle_bank = flip_banks.tile([P, N_IDLE], F32, name="bank")
        turned_w1 = {}
        hidden_acc = {}
        edge_terms = {}

        idle_passes(IDLE_BEFORE_X)
        x_codes, x_scales = quantise(flip(x_rows[:]), keep, "x")
        turn_b1()
        spread_row(0)
        idle_passes(IDLE_AFTER_X)

        for step in range(PAIRS + 2):
            if step < PAIRS:
                for r in range(2):
                    turned_w1[2 * step + r] = flip(w1_rows[step][:, r, 0:NODE])
            if step == PAIRS:
                turned_w2 = flip(w2_rows[:])
                spread_row(1)
            if 1 <= step <= PAIRS:
                multiply(step - 1)
            if step < PAIRS:
                edge_and_bias(step)
            if step >= 2:
                add_edge_terms(step - 2)
                if (step - 2) % HALVES == HALVES - 1:
                    hidden_pass((step - 2) // HALVES)
            if step == PAIRS:
                w2_codes, w2_scales = quantise(turned_w2, keep, "w2")

        for c in range(PASSES):
            cols = slice(c * P, (c + 1) * P)
            nc.tensor.matmul_mx(
                out=out_acc[:],
                lhsT=h_codes[:, cols].bitcast(FP8X4),
                lhsT_scale=h_scales[:, cols],
                rhs=w2_codes[:, cols].bitcast(FP8X4),
                rhs_scale=w2_scales[:, cols],
                start=(c == 0),
                stop=(c == PASSES - 1),
            )

        biased = keep.tile([P, P], F32)
        nc.vector.tensor_tensor(out=biased[:], in0=out_acc[:], in1=spread[:, P : 2 * P], op=ALU.add)
        result = keep.tile([P, P], F32)
        nc.scalar.activation(out=result[:], in_=biased[:], func=ACT.Tanh)
        nc.sync.dma_start(out=out, in_=result[:])
